import numpy as np
import ml_dtypes


def mxq(x, axis, fmt="e4m3"):
    dtype, down = {"e4m3": (ml_dtypes.float8_e4m3fn, 7), "e5m2": (ml_dtypes.float8_e5m2, 14)}[fmt]
    v = np.moveaxis(np.asarray(x, np.float32).astype(ml_dtypes.bfloat16).astype(np.float64), axis, -1)
    blocks = v.reshape(v.shape[:-1] + (-1, 32))
    amax = np.abs(blocks).max(-1, keepdims=True)
    byte = np.maximum(np.where(amax > 0, np.frexp(amax)[1] - 1 + 127, 0) - down, 1)
    scale = np.exp2(byte - 127.0)
    codes = (blocks / scale).astype(np.float32).astype(dtype).astype(np.float64)
    return np.moveaxis((codes * scale).reshape(v.shape), -1, axis)


WIDE = False


def mx_kscale(k):
    if not WIDE:
        return np.ones(k)
    levels = np.array([10, -10, 5, -5, 0])
    if k % 512:
        return np.exp2(np.random.permutation(np.resize(levels, k // 32))).repeat(32)
    a = np.empty((k // 512, 16))
    for p in range(k // 512):
        a[p, :8] = np.random.permutation(np.resize(levels, 8))
        for g in range(8):
            far = levels[np.abs(levels - a[p, g]) >= 10]
            a[p, g + 8] = far[np.random.randint(len(far))]
    return np.exp2(a.ravel()).repeat(32)


BF16 = ml_dtypes.bfloat16


def bf(x):
    return np.asarray(x, np.float32).astype(BF16)


def f64(x):
    return np.asarray(x).astype(np.float64)


B, C, O, ROWS, COLS, KH, KW = 128, 1024, 128, 2, 2, 4, 4
H, W, K = ROWS + KH - 1, COLS + KW - 1, C * KH * KW


def setup_inputs():
    sc = mx_kscale(K)[::KH * KW]
    return {"x": bf(np.random.standard_normal((B, C, H, W)) * sc[None, :, None, None]),
            "weight": bf(np.random.standard_normal((ROWS, COLS, O, C, KH, KW)) / np.sqrt(K) / sc[None, None, None, :, None, None])}


def reference(x, weight):
    x, weight = f64(x), f64(weight)
    rows, cols, o, c, kh, kw = weight.shape
    b = x.shape[0]
    patches = np.stack(
        [np.stack([x[:, :, u:u + rows, v:v + cols] for v in range(kw)], axis=2)
         for u in range(kh)], axis=2)
    p = patches.transpose(4, 5, 0, 1, 2, 3).reshape(rows * cols, b, c * kh * kw)
    w = weight.reshape(rows * cols, o, c * kh * kw)
    y = mxq(p, 2, "e4m3") @ mxq(w, 2, "e4m3").transpose(0, 2, 1)
    return y.reshape(rows, cols, b, o).transpose(2, 3, 0, 1)

@@ -1,0 +1,169 @@
+from contextlib import ExitStack
+
+import concourse.mybir as mybir
+from concourse.masks import make_identity
+
+BF16 = mybir.dt.bfloat16
+F32 = mybir.dt.float32
+U32 = mybir.dt.uint32
+U8 = mybir.dt.uint8
+FP8X4 = mybir.dt.float8_e4m3fn_x4
+
+P = 128
+CHANNELS = 1024
+ROWS = 2
+COLS = 2
+KH = 4
+KW = 4
+HEIGHT = ROWS + KH - 1
+WIDTH = COLS + KW - 1
+POSITIONS = ROWS * COLS
+
+K_PASS = 4 * P
+BANK_WORDS = 512
+UNIT_FLIPS = BANK_WORDS // P
+UNIT_K = 2 * BANK_WORDS
+UNIT_PASSES = UNIT_K // K_PASS
+UNIT_CHANNELS = UNIT_K // (KH * KW)
+UNIT_X = UNIT_CHANNELS * HEIGHT * WIDTH
+ROUND_UNITS = 2
+CHUNK_CHANNELS = ROUND_UNITS * UNIT_CHANNELS
+CHUNKS = CHANNELS // CHUNK_CHANNELS
+ROUNDS = CHUNKS * POSITIONS
+
+VECTOR_EVERY = 16
+
+FLOPS = 2 * POSITIONS * P * P * CHANNELS * KH * KW
+
+
+def tile_localconvolution_k_kernel(tc, x, weight, out):
+    nc = tc.nc
+    with ExitStack() as ctx:
+        const = ctx.enter_context(tc.tile_pool(name="const", bufs=1))
+        inputs = ctx.enter_context(tc.tile_pool(name="inputs", bufs=1))
+        patches = ctx.enter_context(tc.tile_pool(name="patches", bufs=3 * ROUND_UNITS))
+        regrouped = ctx.enter_context(tc.tile_pool(name="regrouped", bufs=2 * ROUND_UNITS))
+        quantised = ctx.enter_context(tc.tile_pool(name="quantised", bufs=3 * ROUND_UNITS))
+        banks = ctx.enter_context(tc.psum_pool(name="banks", bufs=4))
+        sums = ctx.enter_context(tc.psum_pool(name="sums", bufs=1))
+        ctx.enter_context(tc.manual_schedule())
+
+        identity = const.tile([P, P], F32)
+        make_identity(nc, identity[:])
+
+        x_units = []
+        w_rounds = []
+
+        def load_x(c, n):
+            first = c * CHUNK_CHANNELS + n * UNIT_CHANNELS
+            x_sb = inputs.tile([P, UNIT_X], BF16, name="x%d_%d" % (c, n))
+            nc.sync.dma_start(
+                out=x_sb[:], in_=x[:, first : first + UNIT_CHANNELS, :, :].rearrange("b c h w -> b (c h w)")
+            )
+            x_units.append(x_sb)
+
+        def load_w(c, q):
+            first = c * CHUNK_CHANNELS
+            w_sb = inputs.tile([P, ROUND_UNITS * UNIT_K], BF16, name="w%d_%d" % (c, q))
+            nc.sync.dma_start(
+                out=w_sb[:],
+                in_=weight[q // COLS, q % COLS, :, first : first + CHUNK_CHANNELS, :, :].rearrange(
+                    "o c u v -> o (c u v)"
+                ),
+            )
+            w_rounds.append(w_sb)
+
+        for c in range(CHUNKS):
+            load_x(c, 0)
+            load_w(c, 0)
+            load_x(c, 1)
+            for q in range(1, POSITIONS):
+                load_w(c, q)
+
+        totals = [sums.tile([P, P], F32, name="total%d" % q) for q in range(POSITIONS)]
+        planes = const.tile([P, POSITIONS, P], F32)
+
+        def gather(r, n):
+            i = (r % POSITIONS) // COLS
+            j = (r % POSITIONS) % COLS
+            patch = patches.tile([P, UNIT_K], BF16)
+            nc.vector.tensor_copy(
+                out=patch[:].rearrange("b (c u v) -> b c u v", u=KH, v=KW),
+                in_=x_units[(r // POSITIONS) * ROUND_UNITS + n][:].rearrange(
+                    "b (c h w) -> b c h w", h=HEIGHT, w=WIDTH
+                )[:, :, i : i + KH, j : j + KW],
+            )
+            return patch
+
+        def flip(rows, label, bank_index):
+            row_words = rows.bitcast(F32)
+            bank = banks.tile([P, UNIT_FLIPS, P], F32)
+            for f in range(UNIT_FLIPS):
+                g, h = divmod(f, 2)
+                nc.tensor.transpose(
+                    bank[:, f, :], row_words[:, 2 * g * P + h : 2 * (g + 1) * P : 2], identity[:]
+                )
+            grouped = regrouped.tile(
+                [P, UNIT_K], BF16, name=label + "_grouped", tag=label + "_grouped", align_bytes=64
+            )
+            target = grouped[:].bitcast(F32).rearrange("p (g c h) -> p g c h", g=UNIT_PASSES, h=2)
+            source = bank[:].rearrange("p (g h) c -> p g c h", h=2)
+            if bank_index % VECTOR_EVERY == VECTOR_EVERY // 2:
+                nc.vector.tensor_copy(out=target, in_=source)
+            else:
+                nc.scalar.copy(out=target, in_=source)
+            return grouped
+
+        def quantise(grouped, label):
+            codes = quantised.tile(
+                [P, UNIT_K // 4], U32, name=label + "_codes", tag=label + "_codes", align_bytes=64
+            )
+            scales = quantised.tile(
+                [P, UNIT_K // 4], U8, name=label + "_scales", tag=label + "_scales", align_bytes=64
+            )
+            nc.vector.quantize_mx(out=codes[:].bitcast(FP8X4), scales=scales[:], in_=grouped[:])
+            return codes, scales
+
+        def multiply(r, units):
+            total = totals[r % POSITIONS]
+            first_round = r // POSITIONS == 0
+            last_round = r // POSITIONS == CHUNKS - 1
+            for n in range(ROUND_UNITS):
+                (x_codes, x_scales), (w_codes, w_scales) = units[n]
+                for g in range(UNIT_PASSES):
+                    cols = slice(g * P, (g + 1) * P)
+                    nc.tensor.matmul_mx(
+                        out=total[:],
+                        lhsT=x_codes[:, cols].bitcast(FP8X4),
+                        lhsT_scale=x_scales[:, cols],
+                        rhs=w_codes[:, cols].bitcast(FP8X4),
+                        rhs_scale=w_scales[:, cols],
+                        start=(first_round and n == 0 and g == 0),
+                        stop=(last_round and n == ROUND_UNITS - 1 and g == UNIT_PASSES - 1),
+                    )
+            if last_round:
+                nc.vector.tensor_copy(out=planes[:, r % POSITIONS, :], in_=total[:])
+
+        patch_of = {0: [gather(0, n) for n in range(ROUND_UNITS)]}
+        grouped_of = {}
+        mx_of = {}
+        for s in range(ROUNDS + 2):
+            if s + 1 < ROUNDS:
+                patch_of[s + 1] = [gather(s + 1, n) for n in range(ROUND_UNITS)]
+            if s < ROUNDS:
+                grouped_of[s] = []
+                for n in range(ROUND_UNITS):
+                    bank_index = 2 * (s * ROUND_UNITS + n)
+                    x_grouped = flip(patch_of[s][n][:], "x", bank_index)
+                    w_grouped = flip(w_rounds[s][:, n * UNIT_K : (n + 1) * UNIT_K], "w", bank_index + 1)
+                    grouped_of[s].append((x_grouped, w_grouped))
+            if 1 <= s <= ROUNDS:
+                mx_of[s - 1] = [
+                    (quantise(x_grouped, "x"), quantise(w_grouped, "w")) for x_grouped, w_grouped in grouped_of[s - 1]
+                ]
+            if s >= 2:
+                multiply(s - 2, mx_of[s - 2])
+
+        result = const.tile([P, P, POSITIONS], F32)
+        nc.vector.tensor_copy(out=result[:], in_=planes[:].rearrange("b q o -> b o q"))
+        nc.sync.dma_start(out=out.rearrange("b o i j -> b (o i j)"), in_=result[:].rearrange("b o q -> b (o q)"))

@@ -88,10 +88,10 @@ def tile_localconvolution_k_kernel(tc, x, weight, out):
             j = (r % POSITIONS) % COLS
             patch = patches.tile([P, UNIT_K], BF16)
             nc.vector.tensor_copy(
-                out=patch[:].rearrange("b (c u v) -> b c u v", u=KH, v=KW),
+                out=patch[:].rearrange("b (h c u e) -> b h c u e", h=2, u=KH, e=2),
                 in_=x_units[(r // POSITIONS) * ROUND_UNITS + n][:].rearrange(
                     "b (c h w) -> b c h w", h=HEIGHT, w=WIDTH
-                )[:, :, i : i + KH, j : j + KW],
+                )[:, :, i : i + KH, j : j + KW].rearrange("b c u (h e) -> b h c u e", e=2),
             )
             return patch
 
@@ -100,9 +100,11 @@ def tile_localconvolution_k_kernel(tc, x, weight, out):
             bank = banks.tile([P, UNIT_FLIPS, P], F32)
             for f in range(UNIT_FLIPS):
                 g, h = divmod(f, 2)
-                nc.tensor.transpose(
-                    bank[:, f, :], row_words[:, 2 * g * P + h : 2 * (g + 1) * P : 2], identity[:]
-                )
+                if label == "x":
+                    words = row_words[:, (h * UNIT_PASSES + g) * P : (h * UNIT_PASSES + g + 1) * P]
+                else:
+                    words = row_words[:, 2 * g * P + h : 2 * (g + 1) * P : 2]
+                nc.tensor.transpose(bank[:, f, :], words, identity[:])
             grouped = regrouped.tile(
                 [P, UNIT_K], BF16, name=label + "_grouped", tag=label + "_grouped", align_bytes=64
             )

@@ -25,13 +25,11 @@ UNIT_FLIPS = BANK_WORDS // P
 UNIT_K = 2 * BANK_WORDS
 UNIT_PASSES = UNIT_K // K_PASS
 UNIT_CHANNELS = UNIT_K // (KH * KW)
-UNIT_X = UNIT_CHANNELS * HEIGHT * WIDTH
 ROUND_UNITS = 2
+ROUND_K = ROUND_UNITS * UNIT_K
 CHUNK_CHANNELS = ROUND_UNITS * UNIT_CHANNELS
 CHUNKS = CHANNELS // CHUNK_CHANNELS
-ROUNDS = CHUNKS * POSITIONS
-
-VECTOR_EVERY = 16
+X_ROW = HEIGHT * WIDTH
 
 FLOPS = 2 * POSITIONS * P * P * CHANNELS * KH * KW
 
@@ -41,128 +39,153 @@ def tile_localconvolution_k_kernel(tc, x, weight, out):
     with ExitStack() as ctx:
         const = ctx.enter_context(tc.tile_pool(name="const", bufs=1))
         inputs = ctx.enter_context(tc.tile_pool(name="inputs", bufs=1))
-        patches = ctx.enter_context(tc.tile_pool(name="patches", bufs=3 * ROUND_UNITS))
-        regrouped = ctx.enter_context(tc.tile_pool(name="regrouped", bufs=2 * ROUND_UNITS))
-        quantised = ctx.enter_context(tc.tile_pool(name="quantised", bufs=3 * ROUND_UNITS))
-        banks = ctx.enter_context(tc.psum_pool(name="banks", bufs=4))
+        w_pool = ctx.enter_context(tc.tile_pool(name="w_pool", bufs=20))
+        patches = ctx.enter_context(tc.tile_pool(name="patches", bufs=3))
+        regrouped = ctx.enter_context(tc.tile_pool(name="regrouped", bufs=2))
+        quantised = ctx.enter_context(tc.tile_pool(name="quantised", bufs=3))
+        banks = ctx.enter_context(tc.psum_pool(name="banks", bufs=6))
         sums = ctx.enter_context(tc.psum_pool(name="sums", bufs=1))
         ctx.enter_context(tc.manual_schedule())
 
         identity = const.tile([P, P], F32)
         make_identity(nc, identity[:])
 
-        x_units = []
-        w_rounds = []
+        HALF = COLS
+        order = [(c, half + q) for half in range(0, POSITIONS, HALF) for c in range(CHUNKS) for q in range(HALF)]
+        rounds = len(order)
+        x_of = {}
+        w_of = {}
 
-        def load_x(c, n):
+        def load_x(c, n, parts=1):
+            if n == 0:
+                x_of[c] = inputs.tile([P, CHUNK_CHANNELS * X_ROW], BF16, name="x%d" % c)
             first = c * CHUNK_CHANNELS + n * UNIT_CHANNELS
-            x_sb = inputs.tile([P, UNIT_X], BF16, name="x%d_%d" % (c, n))
+            count = UNIT_CHANNELS
             nc.sync.dma_start(
-                out=x_sb[:], in_=x[:, first : first + UNIT_CHANNELS, :, :].rearrange("b c h w -> b (c h w)")
+                out=x_of[c][:, n * UNIT_CHANNELS * X_ROW : (n + 1) * UNIT_CHANNELS * X_ROW],
+                in_=x[:, first : first + count, :, :].rearrange("b c h w -> b (c h w)"),
             )
-            x_units.append(x_sb)
 
-        def load_w(c, q):
-            first = c * CHUNK_CHANNELS
-            w_sb = inputs.tile([P, ROUND_UNITS * UNIT_K], BF16, name="w%d_%d" % (c, q))
-            nc.sync.dma_start(
-                out=w_sb[:],
-                in_=weight[q // COLS, q % COLS, :, first : first + CHUNK_CHANNELS, :, :].rearrange(
-                    "o c u v -> o (c u v)"
-                ),
-            )
-            w_rounds.append(w_sb)
+        def load_w(r, split):
+            c, q = order[r]
+            w_sb = w_pool.tile([P, ROUND_K], BF16, name="w%d" % r, tag="w")
+            per = ROUND_UNITS // split
+            for n in range(split):
+                first = c * CHUNK_CHANNELS + n * per * UNIT_CHANNELS
+                nc.sync.dma_start(
+                    out=w_sb[:, n * per * UNIT_K : (n + 1) * per * UNIT_K],
+                    in_=weight[q // COLS, q % COLS, :, first : first + per * UNIT_CHANNELS, :, :].rearrange(
+                        "o c u v -> o (c u v)"
+                    ),
+                )
+            w_of[r] = w_sb
 
-        for c in range(CHUNKS):
-            load_x(c, 0)
-            load_w(c, 0)
-            load_x(c, 1)
-            for q in range(1, POSITIONS):
-                load_w(c, q)
+        for r in range(rounds):
+            c, q = order[r]
+            if c not in x_of:
+                load_x(c, 0)
+                if r == 0:
+                    load_w(0, 2)
+                load_x(c, 1)
+            if r > 0:
+                load_w(r, 1)
 
-        totals = [sums.tile([P, P], F32, name="total%d" % q) for q in range(POSITIONS)]
         planes = const.tile([P, POSITIONS, P], F32)
+        totals = {}
 
-        def gather(r, n):
-            i = (r % POSITIONS) // COLS
-            j = (r % POSITIONS) % COLS
-            patch = patches.tile([P, UNIT_K], BF16)
-            nc.vector.tensor_copy(
-                out=patch[:].rearrange("b (h c u e) -> b h c u e", h=2, u=KH, e=2),
-                in_=x_units[(r // POSITIONS) * ROUND_UNITS + n][:].rearrange(
-                    "b (c h w) -> b c h w", h=HEIGHT, w=WIDTH
-                )[:, :, i : i + KH, j : j + KW].rearrange("b c u (h e) -> b h c u e", e=2),
-            )
+        def gather_part(engine, patch, r, lo, hi):
+            c, q = order[r]
+            i, j = q // COLS, q % COLS
+            target = patch[:].rearrange("b (h c u e) -> b h c u e", h=2, u=KH, e=2)[:, :, lo:hi]
+            source = x_of[c][:].rearrange("b (c h w) -> b c h w", h=HEIGHT, w=WIDTH)[
+                :, lo:hi, i : i + KH, j : j + KW
+            ].rearrange("b c u (h e) -> b h c u e", e=2)
+
+            if engine == "vector":
+                nc.vector.tensor_copy(out=target, in_=source)
+            elif engine == "scalar":
+                nc.scalar.copy(out=target, in_=source)
+            else:
+                nc.gpsimd.tensor_scalar(
+                    out=target, in0=source, scalar1=1.0, scalar2=0.0, op0=mybir.AluOpType.mult, op1=mybir.AluOpType.add
+                )
+
+        def gather(r):
+            patch = patches.tile([P, ROUND_K], BF16, name="patch", tag="patch")
+            if r == 0:
+                gather_part("vector", patch, r, 0, UNIT_CHANNELS)
+                gather_part("vector", patch, r, UNIT_CHANNELS, CHUNK_CHANNELS)
+            else:
+                gather_part("vector", patch, r, 0, CHUNK_CHANNELS)
             return patch
 
-        def flip(rows, label, bank_index):
-            row_words = rows.bitcast(F32)
+        def flip(words, grouped, engine):
             bank = banks.tile([P, UNIT_FLIPS, P], F32)
             for f in range(UNIT_FLIPS):
-                g, h = divmod(f, 2)
-                if label == "x":
-                    words = row_words[:, (h * UNIT_PASSES + g) * P : (h * UNIT_PASSES + g + 1) * P]
-                else:
-                    words = row_words[:, 2 * g * P + h : 2 * (g + 1) * P : 2]
-                nc.tensor.transpose(bank[:, f, :], words, identity[:])
-            grouped = regrouped.tile(
-                [P, UNIT_K], BF16, name=label + "_grouped", tag=label + "_grouped", align_bytes=64
-            )
-            target = grouped[:].bitcast(F32).rearrange("p (g c h) -> p g c h", g=UNIT_PASSES, h=2)
+                nc.tensor.transpose(bank[:, f, :], words[f], identity[:])
+            target = grouped.bitcast(F32).rearrange("p (g c h) -> p g c h", g=UNIT_PASSES, h=2)
             source = bank[:].rearrange("p (g h) c -> p g c h", h=2)
-            if bank_index % VECTOR_EVERY == VECTOR_EVERY // 2:
+            if engine == "vector":
                 nc.vector.tensor_copy(out=target, in_=source)
             else:
                 nc.scalar.copy(out=target, in_=source)
-            return grouped
+
+        def flips(r, patch):
+            x_grouped = regrouped.tile([P, ROUND_K], BF16, name="x_grouped", tag="x_grouped", align_bytes=64)
+            w_grouped = regrouped.tile([P, ROUND_K], BF16, name="w_grouped", tag="w_grouped", align_bytes=64)
+            x_words = patch[:].bitcast(F32)
+            w_words = w_of[r][:].bitcast(F32)
+            for n in range(ROUND_UNITS):
+                ks = slice(n * UNIT_K, (n + 1) * UNIT_K)
+                passes = [n * UNIT_PASSES + f // 2 for f in range(UNIT_FLIPS)]
+                flip(
+                    [x_words[:, (f % 2) * ROUND_K // 4 + g * P : (f % 2) * ROUND_K // 4 + (g + 1) * P] for f, g in enumerate(passes)],
+                    x_grouped[:, ks],
+                    "scalar",
+                )
+                flip(
+                    [w_words[:, 2 * g * P + f % 2 : 2 * (g + 1) * P : 2] for f, g in enumerate(passes)],
+                    w_grouped[:, ks],
+                    "scalar",
+                )
+            return x_grouped, w_grouped
 
         def quantise(grouped, label):
-            codes = quantised.tile(
-                [P, UNIT_K // 4], U32, name=label + "_codes", tag=label + "_codes", align_bytes=64
-            )
-            scales = quantised.tile(
-                [P, UNIT_K // 4], U8, name=label + "_scales", tag=label + "_scales", align_bytes=64
-            )
+            codes = quantised.tile([P, ROUND_K // 4], U32, name=label + "_codes", tag=label + "_codes", align_bytes=64)
+            scales = quantised.tile([P, ROUND_K // 4], U8, name=label + "_scales", tag=label + "_scales", align_bytes=64)
             nc.vector.quantize_mx(out=codes[:].bitcast(FP8X4), scales=scales[:], in_=grouped[:])
             return codes, scales
 
-        def multiply(r, units):
-            total = totals[r % POSITIONS]
-            first_round = r // POSITIONS == 0
-            last_round = r // POSITIONS == CHUNKS - 1
-            for n in range(ROUND_UNITS):
-                (x_codes, x_scales), (w_codes, w_scales) = units[n]
-                for g in range(UNIT_PASSES):
-                    cols = slice(g * P, (g + 1) * P)
-                    nc.tensor.matmul_mx(
-                        out=total[:],
-                        lhsT=x_codes[:, cols].bitcast(FP8X4),
-                        lhsT_scale=x_scales[:, cols],
-                        rhs=w_codes[:, cols].bitcast(FP8X4),
-                        rhs_scale=w_scales[:, cols],
-                        start=(first_round and n == 0 and g == 0),
-                        stop=(last_round and n == ROUND_UNITS - 1 and g == UNIT_PASSES - 1),
-                    )
-            if last_round:
-                nc.vector.tensor_copy(out=planes[:, r % POSITIONS, :], in_=total[:])
+        def multiply(r, mx):
+            c, q = order[r]
+            (x_codes, x_scales), (w_codes, w_scales) = mx
+            if c == 0:
+                totals[q] = sums.tile([P, P], F32, name="total", tag="total%d" % (q % HALF))
+            for g in range(ROUND_K // K_PASS):
+                cols = slice(g * P, (g + 1) * P)
+                nc.tensor.matmul_mx(
+                    out=totals[q][:],
+                    lhsT=x_codes[:, cols].bitcast(FP8X4),
+                    lhsT_scale=x_scales[:, cols],
+                    rhs=w_codes[:, cols].bitcast(FP8X4),
+                    rhs_scale=w_scales[:, cols],
+                    start=(c == 0 and g == 0),
+                    stop=(c == CHUNKS - 1 and g == ROUND_K // K_PASS - 1),
+                )
+            if c == CHUNKS - 1:
+                nc.vector.tensor_copy(out=planes[:, q, :], in_=totals[q][:])
 
-        patch_of = {0: [gather(0, n) for n in range(ROUND_UNITS)]}
+        patch_of = {0: gather(0)}
         grouped_of = {}
         mx_of = {}
-        for s in range(ROUNDS + 2):
-            if s + 1 < ROUNDS:
-                patch_of[s + 1] = [gather(s + 1, n) for n in range(ROUND_UNITS)]
-            if s < ROUNDS:
-                grouped_of[s] = []
-                for n in range(ROUND_UNITS):
-                    bank_index = 2 * (s * ROUND_UNITS + n)
-                    x_grouped = flip(patch_of[s][n][:], "x", bank_index)
-                    w_grouped = flip(w_rounds[s][:, n * UNIT_K : (n + 1) * UNIT_K], "w", bank_index + 1)
-                    grouped_of[s].append((x_grouped, w_grouped))
-            if 1 <= s <= ROUNDS:
-                mx_of[s - 1] = [
-                    (quantise(x_grouped, "x"), quantise(w_grouped, "w")) for x_grouped, w_grouped in grouped_of[s - 1]
-                ]
+        for s in range(rounds + 2):
+            if s + 1 < rounds:
+                patch_of[s + 1] = gather(s + 1)
+            if s < rounds:
+                grouped_of[s] = flips(s, patch_of[s])
+            if 1 <= s <= rounds:
+                x_grouped, w_grouped = grouped_of[s - 1]
+                mx_of[s - 1] = (quantise(x_grouped, "x"), quantise(w_grouped, "w"))
             if s >= 2:
                 multiply(s - 2, mx_of[s - 2])
 

@@ -99,8 +99,8 @@ def tile_localconvolution_k_kernel(tc, x, weight, out):
             target = patch[:].rearrange("b (h c u e) -> b h c u e", h=2, u=KH, e=2)[:, :, lo:hi]
             source = x_of[c][:].rearrange("b (c h w) -> b c h w", h=HEIGHT, w=WIDTH)[
                 :, lo:hi, i : i + KH, j : j + KW
-            ].rearrange("b c u (h e) -> b h c u e", e=2)
-
+            ].rearrange("b c u (h e) -> b c u h e", e=2)
+            target = target.rearrange("b h c u e -> b c u h e")
             if engine == "vector":
                 nc.vector.tensor_copy(out=target, in_=source)
             elif engine == "scalar":

@@ -92,6 +92,7 @@ def tile_localconvolution_k_kernel(tc, x, weight, out):
 
         planes = const.tile([P, POSITIONS, P], F32)
         totals = {}
+        late = []
 
         def gather_part(engine, patch, r, lo, hi):
             c, q = order[r]
@@ -126,7 +127,7 @@ def tile_localconvolution_k_kernel(tc, x, weight, out):
             target = grouped.bitcast(F32).rearrange("p (g c h) -> p g c h", g=UNIT_PASSES, h=2)
             source = bank[:].rearrange("p (g h) c -> p g c h", h=2)
             if engine == "vector":
-                nc.vector.tensor_copy(out=target, in_=source)
+                late.append((target, source))
             else:
                 nc.scalar.copy(out=target, in_=source)
 
@@ -146,7 +147,7 @@ def tile_localconvolution_k_kernel(tc, x, weight, out):
                 flip(
                     [w_words[:, 2 * g * P + f % 2 : 2 * (g + 1) * P : 2] for f, g in enumerate(passes)],
                     w_grouped[:, ks],
-                    "scalar",
+                    "vector" if n == 1 and r % 2 == 1 else "scalar",
                 )
             return x_grouped, w_grouped
 
@@ -186,6 +187,9 @@ def tile_localconvolution_k_kernel(tc, x, weight, out):
             if 1 <= s <= rounds:
                 x_grouped, w_grouped = grouped_of[s - 1]
                 mx_of[s - 1] = (quantise(x_grouped, "x"), quantise(w_grouped, "w"))
+            for target, source in late:
+                nc.vector.tensor_copy(out=target, in_=source)
+            late.clear()
             if s >= 2:
                 multiply(s - 2, mx_of[s - 2])
 

@@ -41,7 +41,7 @@ def tile_localconvolution_k_kernel(tc, x, weight, out):
         inputs = ctx.enter_context(tc.tile_pool(name="inputs", bufs=1))
         w_pool = ctx.enter_context(tc.tile_pool(name="w_pool", bufs=20))
         patches = ctx.enter_context(tc.tile_pool(name="patches", bufs=3))
-        regrouped = ctx.enter_context(tc.tile_pool(name="regrouped", bufs=2))
+        regrouped = ctx.enter_context(tc.tile_pool(name="regrouped", bufs=3))
         quantised = ctx.enter_context(tc.tile_pool(name="quantised", bufs=3))
         banks = ctx.enter_context(tc.psum_pool(name="banks", bufs=6))
         sums = ctx.enter_context(tc.psum_pool(name="sums", bufs=1))
@@ -59,12 +59,14 @@ def tile_localconvolution_k_kernel(tc, x, weight, out):
         def load_x(c, n, parts=1):
             if n == 0:
                 x_of[c] = inputs.tile([P, CHUNK_CHANNELS * X_ROW], BF16, name="x%d" % c)
-            first = c * CHUNK_CHANNELS + n * UNIT_CHANNELS
-            count = UNIT_CHANNELS
-            nc.sync.dma_start(
-                out=x_of[c][:, n * UNIT_CHANNELS * X_ROW : (n + 1) * UNIT_CHANNELS * X_ROW],
-                in_=x[:, first : first + count, :, :].rearrange("b c h w -> b (c h w)"),
-            )
+            count = UNIT_CHANNELS // parts
+            for m in range(parts):
+                lo = n * UNIT_CHANNELS + m * count
+                first = c * CHUNK_CHANNELS + lo
+                nc.sync.dma_start(
+                    out=x_of[c][:, lo * X_ROW : (lo + count) * X_ROW],
+                    in_=x[:, first : first + count, :, :].rearrange("b c h w -> b (c h w)"),
+                )
 
         def load_w(r, split):
             c, q = order[r]
@@ -83,7 +85,7 @@ def tile_localconvolution_k_kernel(tc, x, weight, out):
         for r in range(rounds):
             c, q = order[r]
             if c not in x_of:
-                load_x(c, 0)
+                load_x(c, 0, 2 if r == 0 else 1)
                 if r == 0:
                     load_w(0, 2)
                 load_x(c, 1)
@@ -114,7 +116,8 @@ def tile_localconvolution_k_kernel(tc, x, weight, out):
         def gather(r):
             patch = patches.tile([P, ROUND_K], BF16, name="patch", tag="patch")
             if r == 0:
-                gather_part("vector", patch, r, 0, UNIT_CHANNELS)
+                gather_part("vector", patch, r, 0, UNIT_CHANNELS // 2)
+                gather_part("vector", patch, r, UNIT_CHANNELS // 2, UNIT_CHANNELS)
                 gather_part("vector", patch, r, UNIT_CHANNELS, CHUNK_CHANNELS)
             else:
                 gather_part("vector", patch, r, 0, CHUNK_CHANNELS)
@@ -132,8 +135,9 @@ def tile_localconvolution_k_kernel(tc, x, weight, out):
                 nc.scalar.copy(out=target, in_=source)
 
         def flips(r, patch):
-            x_grouped = regrouped.tile([P, ROUND_K], BF16, name="x_grouped", tag="x_grouped", align_bytes=64)
-            w_grouped = regrouped.tile([P, ROUND_K], BF16, name="w_grouped", tag="w_grouped", align_bytes=64)
+            grouped = regrouped.tile([P, 2 * ROUND_K], BF16, name="grouped", tag="grouped", align_bytes=64)
+            x_grouped = grouped[:, :ROUND_K]
+            w_grouped = grouped[:, ROUND_K:]
             x_words = patch[:].bitcast(F32)
             w_words = w_of[r][:].bitcast(F32)
             for n in range(ROUND_UNITS):
@@ -147,29 +151,35 @@ def tile_localconvolution_k_kernel(tc, x, weight, out):
                 flip(
                     [w_words[:, 2 * g * P + f % 2 : 2 * (g + 1) * P : 2] for f, g in enumerate(passes)],
                     w_grouped[:, ks],
-                    "vector" if n == 1 and r % 2 == 1 else "scalar",
+                    "vector" if n == 1 and r % 4 == 1 else "scalar",
                 )
-            return x_grouped, w_grouped
+            return grouped
 
-        def quantise(grouped, label):
-            codes = quantised.tile([P, ROUND_K // 4], U32, name=label + "_codes", tag=label + "_codes", align_bytes=64)
-            scales = quantised.tile([P, ROUND_K // 4], U8, name=label + "_scales", tag=label + "_scales", align_bytes=64)
-            nc.vector.quantize_mx(out=codes[:].bitcast(FP8X4), scales=scales[:], in_=grouped[:])
+        def quantise(grouped, parts):
+            codes = quantised.tile([P, ROUND_K // 2], U32, name="codes", tag="codes", align_bytes=64)
+            scales = quantised.tile([P, ROUND_K // 2], U8, name="scales", tag="scales", align_bytes=64)
+            for first, count in parts:
+                nc.vector.quantize_mx(
+                    out=codes[:, first // 4 : (first + count) // 4].bitcast(FP8X4),
+                    scales=scales[:, first // 4 : (first + count) // 4],
+                    in_=grouped[:, first : first + count],
+                )
             return codes, scales
 
         def multiply(r, mx):
             c, q = order[r]
-            (x_codes, x_scales), (w_codes, w_scales) = mx
+            codes, scales = mx
             if c == 0:
                 totals[q] = sums.tile([P, P], F32, name="total", tag="total%d" % (q % HALF))
             for g in range(ROUND_K // K_PASS):
-                cols = slice(g * P, (g + 1) * P)
+                x_cols = slice(g * P, (g + 1) * P)
+                w_cols = slice(ROUND_K // 4 + g * P, ROUND_K // 4 + (g + 1) * P)
                 nc.tensor.matmul_mx(
                     out=totals[q][:],
-                    lhsT=x_codes[:, cols].bitcast(FP8X4),
-                    lhsT_scale=x_scales[:, cols],
-                    rhs=w_codes[:, cols].bitcast(FP8X4),
-                    rhs_scale=w_scales[:, cols],
+                    lhsT=codes[:, x_cols].bitcast(FP8X4),
+                    lhsT_scale=scales[:, x_cols],
+                    rhs=codes[:, w_cols].bitcast(FP8X4),
+                    rhs_scale=scales[:, w_cols],
                     start=(c == 0 and g == 0),
                     stop=(c == CHUNKS - 1 and g == ROUND_K // K_PASS - 1),
                 )
@@ -185,8 +195,11 @@ def tile_localconvolution_k_kernel(tc, x, weight, out):
             if s < rounds:
                 grouped_of[s] = flips(s, patch_of[s])
             if 1 <= s <= rounds:
-                x_grouped, w_grouped = grouped_of[s - 1]
-                mx_of[s - 1] = (quantise(x_grouped, "x"), quantise(w_grouped, "w"))
+                if s < rounds:
+                    parts = [(0, 2 * ROUND_K)]
+                else:
+                    parts = [(first, UNIT_K) for n in range(ROUND_UNITS) for first in (n * UNIT_K, ROUND_K + n * UNIT_K)]
+                mx_of[s - 1] = quantise(grouped_of[s - 1], parts)
             for target, source in late:
                 nc.vector.tensor_copy(out=target, in_=source)
             late.clear()
@@ -194,5 +207,7 @@ def tile_localconvolution_k_kernel(tc, x, weight, out):
                 multiply(s - 2, mx_of[s - 2])
 
         result = const.tile([P, P, POSITIONS], F32)
-        nc.vector.tensor_copy(out=result[:], in_=planes[:].rearrange("b q o -> b o q"))
+        for lo, copy in ((0, nc.vector.tensor_copy), (P // 2, nc.scalar.copy)):
+            hi = lo + P // 2
+            copy(out=result[:, lo:hi, :], in_=planes[:, :, lo:hi].rearrange("b q o -> b o q"))
         nc.sync.dma_start(out=out.rearrange("b o i j -> b (o i j)"), in_=result[:].rearrange("b o q -> b (o q)"))

@@ -39,10 +39,10 @@ def tile_localconvolution_k_kernel(tc, x, weight, out):
     with ExitStack() as ctx:
         const = ctx.enter_context(tc.tile_pool(name="const", bufs=1))
         inputs = ctx.enter_context(tc.tile_pool(name="inputs", bufs=1))
-        w_pool = ctx.enter_context(tc.tile_pool(name="w_pool", bufs=20))
+        w_pool = ctx.enter_context(tc.tile_pool(name="w_pool", bufs=18))
         patches = ctx.enter_context(tc.tile_pool(name="patches", bufs=3))
-        regrouped = ctx.enter_context(tc.tile_pool(name="regrouped", bufs=3))
-        quantised = ctx.enter_context(tc.tile_pool(name="quantised", bufs=3))
+        regrouped = ctx.enter_context(tc.tile_pool(name="regrouped", bufs=4))
+        quantised = ctx.enter_context(tc.tile_pool(name="quantised", bufs=6))
         banks = ctx.enter_context(tc.psum_pool(name="banks", bufs=6))
         sums = ctx.enter_context(tc.psum_pool(name="sums", bufs=1))
         ctx.enter_context(tc.manual_schedule())
@@ -189,22 +189,23 @@ def tile_localconvolution_k_kernel(tc, x, weight, out):
         patch_of = {0: gather(0)}
         grouped_of = {}
         mx_of = {}
-        for s in range(rounds + 2):
+        for s in range(rounds + 4):
             if s + 1 < rounds:
                 patch_of[s + 1] = gather(s + 1)
             if s < rounds:
                 grouped_of[s] = flips(s, patch_of[s])
-            if 1 <= s <= rounds:
-                if s < rounds:
+            if 2 <= s < rounds + 2:
+                if s - 2 < rounds - 1:
                     parts = [(0, 2 * ROUND_K)]
                 else:
                     parts = [(first, UNIT_K) for n in range(ROUND_UNITS) for first in (n * UNIT_K, ROUND_K + n * UNIT_K)]
-                mx_of[s - 1] = quantise(grouped_of[s - 1], parts)
+                mx_of[s - 2] = quantise(grouped_of[s - 2], parts)
             for target, source in late:
                 nc.vector.tensor_copy(out=target, in_=source)
             late.clear()
-            if s >= 2:
-                multiply(s - 2, mx_of[s - 2])
+            if s >= 5 and s % 2 == 1:
+                multiply(s - 5, mx_of[s - 5])
+                multiply(s - 4, mx_of[s - 4])
 
         result = const.tile([P, P, POSITIONS], F32)
         for lo, copy in ((0, nc.vector.tensor_copy), (P // 2, nc.scalar.copy)):

from contextlib import ExitStack

import concourse.mybir as mybir
from concourse.masks import make_identity

BF16 = mybir.dt.bfloat16
F32 = mybir.dt.float32
U32 = mybir.dt.uint32
U8 = mybir.dt.uint8
FP8X4 = mybir.dt.float8_e4m3fn_x4

P = 128
CHANNELS = 1024
ROWS = 2
COLS = 2
KH = 4
KW = 4
HEIGHT = ROWS + KH - 1
WIDTH = COLS + KW - 1
POSITIONS = ROWS * COLS

K_PASS = 4 * P
BANK_WORDS = 512
UNIT_FLIPS = BANK_WORDS // P
UNIT_K = 2 * BANK_WORDS
UNIT_PASSES = UNIT_K // K_PASS
UNIT_CHANNELS = UNIT_K // (KH * KW)
ROUND_UNITS = 2
ROUND_K = ROUND_UNITS * UNIT_K
CHUNK_CHANNELS = ROUND_UNITS * UNIT_CHANNELS
CHUNKS = CHANNELS // CHUNK_CHANNELS
X_ROW = HEIGHT * WIDTH

FLOPS = 2 * POSITIONS * P * P * CHANNELS * KH * KW


def tile_localconvolution_k_kernel(tc, x, weight, out):
    nc = tc.nc
    with ExitStack() as ctx:
        const = ctx.enter_context(tc.tile_pool(name="const", bufs=1))
        inputs = ctx.enter_context(tc.tile_pool(name="inputs", bufs=1))
        w_pool = ctx.enter_context(tc.tile_pool(name="w_pool", bufs=18))
        patches = ctx.enter_context(tc.tile_pool(name="patches", bufs=3))
        regrouped = ctx.enter_context(tc.tile_pool(name="regrouped", bufs=4))
        quantised = ctx.enter_context(tc.tile_pool(name="quantised", bufs=6))
        banks = ctx.enter_context(tc.psum_pool(name="banks", bufs=6))
        sums = ctx.enter_context(tc.psum_pool(name="sums", bufs=1))
        ctx.enter_context(tc.manual_schedule())

        identity = const.tile([P, P], F32)
        make_identity(nc, identity[:])

        HALF = COLS
        order = [(c, half + q) for half in range(0, POSITIONS, HALF) for c in range(CHUNKS) for q in range(HALF)]
        rounds = len(order)
        x_of = {}
        w_of = {}

        def load_x(c, n, parts=1):
            if n == 0:
                x_of[c] = inputs.tile([P, CHUNK_CHANNELS * X_ROW], BF16, name="x%d" % c)
            count = UNIT_CHANNELS // parts
            for m in range(parts):
                lo = n * UNIT_CHANNELS + m * count
                first = c * CHUNK_CHANNELS + lo
                nc.sync.dma_start(
                    out=x_of[c][:, lo * X_ROW : (lo + count) * X_ROW],
                    in_=x[:, first : first + count, :, :].rearrange("b c h w -> b (c h w)"),
                )

        def load_w(r, split):
            c, q = order[r]
            w_sb = w_pool.tile([P, ROUND_K], BF16, name="w%d" % r, tag="w")
            per = ROUND_UNITS // split
            for n in range(split):
                first = c * CHUNK_CHANNELS + n * per * UNIT_CHANNELS
                nc.sync.dma_start(
                    out=w_sb[:, n * per * UNIT_K : (n + 1) * per * UNIT_K],
                    in_=weight[q // COLS, q % COLS, :, first : first + per * UNIT_CHANNELS, :, :].rearrange(
                        "o c u v -> o (c u v)"
                    ),
                )
            w_of[r] = w_sb

        for r in range(rounds):
            c, q = order[r]
            if c not in x_of:
                load_x(c, 0, 2 if r == 0 else 1)
                if r == 0:
                    load_w(0, 2)
                load_x(c, 1)
            if r > 0:
                load_w(r, 1)

        planes = const.tile([P, POSITIONS, P], F32)
        totals = {}
        late = []

        def gather_part(engine, patch, r, lo, hi):
            c, q = order[r]
            i, j = q // COLS, q % COLS
            target = patch[:].rearrange("b (h c u e) -> b h c u e", h=2, u=KH, e=2)[:, :, lo:hi]
            source = x_of[c][:].rearrange("b (c h w) -> b c h w", h=HEIGHT, w=WIDTH)[
                :, lo:hi, i : i + KH, j : j + KW
            ].rearrange("b c u (h e) -> b c u h e", e=2)
            target = target.rearrange("b h c u e -> b c u h e")
            if engine == "vector":
                nc.vector.tensor_copy(out=target, in_=source)
            elif engine == "scalar":
                nc.scalar.copy(out=target, in_=source)
            else:
                nc.gpsimd.tensor_scalar(
                    out=target, in0=source, scalar1=1.0, scalar2=0.0, op0=mybir.AluOpType.mult, op1=mybir.AluOpType.add
                )

        def gather(r):
            patch = patches.tile([P, ROUND_K], BF16, name="patch", tag="patch")
            if r == 0:
                gather_part("vector", patch, r, 0, UNIT_CHANNELS // 2)
                gather_part("vector", patch, r, UNIT_CHANNELS // 2, UNIT_CHANNELS)
                gather_part("vector", patch, r, UNIT_CHANNELS, CHUNK_CHANNELS)
            else:
                gather_part("vector", patch, r, 0, CHUNK_CHANNELS)
            return patch

        def flip(words, grouped, engine):
            bank = banks.tile([P, UNIT_FLIPS, P], F32)
            for f in range(UNIT_FLIPS):
                nc.tensor.transpose(bank[:, f, :], words[f], identity[:])
            target = grouped.bitcast(F32).rearrange("p (g c h) -> p g c h", g=UNIT_PASSES, h=2)
            source = bank[:].rearrange("p (g h) c -> p g c h", h=2)
            if engine == "vector":
                late.append((target, source))
            else:
                nc.scalar.copy(out=target, in_=source)

        def flips(r, patch):
            grouped = regrouped.tile([P, 2 * ROUND_K], BF16, name="grouped", tag="grouped", align_bytes=64)
            x_grouped = grouped[:, :ROUND_K]
            w_grouped = grouped[:, ROUND_K:]
            x_words = patch[:].bitcast(F32)
            w_words = w_of[r][:].bitcast(F32)
            for n in range(ROUND_UNITS):
                ks = slice(n * UNIT_K, (n + 1) * UNIT_K)
                passes = [n * UNIT_PASSES + f // 2 for f in range(UNIT_FLIPS)]
                flip(
                    [x_words[:, (f % 2) * ROUND_K // 4 + g * P : (f % 2) * ROUND_K // 4 + (g + 1) * P] for f, g in enumerate(passes)],
                    x_grouped[:, ks],
                    "scalar",
                )
                flip(
                    [w_words[:, 2 * g * P + f % 2 : 2 * (g + 1) * P : 2] for f, g in enumerate(passes)],
                    w_grouped[:, ks],
                    "vector" if n == 1 and r % 4 == 1 else "scalar",
                )
            return grouped

        def quantise(grouped, parts):
            codes = quantised.tile([P, ROUND_K // 2], U32, name="codes", tag="codes", align_bytes=64)
            scales = quantised.tile([P, ROUND_K // 2], U8, name="scales", tag="scales", align_bytes=64)
            for first, count in parts:
                nc.vector.quantize_mx(
                    out=codes[:, first // 4 : (first + count) // 4].bitcast(FP8X4),
                    scales=scales[:, first // 4 : (first + count) // 4],
                    in_=grouped[:, first : first + count],
                )
            return codes, scales

        def multiply(r, mx):
            c, q = order[r]
            codes, scales = mx
            if c == 0:
                totals[q] = sums.tile([P, P], F32, name="total", tag="total%d" % (q % HALF))
            for g in range(ROUND_K // K_PASS):
                x_cols = slice(g * P, (g + 1) * P)
                w_cols = slice(ROUND_K // 4 + g * P, ROUND_K // 4 + (g + 1) * P)
                nc.tensor.matmul_mx(
                    out=totals[q][:],
                    lhsT=codes[:, x_cols].bitcast(FP8X4),
                    lhsT_scale=scales[:, x_cols],
                    rhs=codes[:, w_cols].bitcast(FP8X4),
                    rhs_scale=scales[:, w_cols],
                    start=(c == 0 and g == 0),
                    stop=(c == CHUNKS - 1 and g == ROUND_K // K_PASS - 1),
                )
            if c == CHUNKS - 1:
                nc.vector.tensor_copy(out=planes[:, q, :], in_=totals[q][:])

        patch_of = {0: gather(0)}
        grouped_of = {}
        mx_of = {}
        for s in range(rounds + 4):
            if s + 1 < rounds:
                patch_of[s + 1] = gather(s + 1)
            if s < rounds:
                grouped_of[s] = flips(s, patch_of[s])
            if 2 <= s < rounds + 2:
                if s - 2 < rounds - 1:
                    parts = [(0, 2 * ROUND_K)]
                else:
                    parts = [(first, UNIT_K) for n in range(ROUND_UNITS) for first in (n * UNIT_K, ROUND_K + n * UNIT_K)]
                mx_of[s - 2] = quantise(grouped_of[s - 2], parts)
            for target, source in late:
                nc.vector.tensor_copy(out=target, in_=source)
            late.clear()
            if s >= 5 and s % 2 == 1:
                multiply(s - 5, mx_of[s - 5])
                multiply(s - 4, mx_of[s - 4])

        result = const.tile([P, P, POSITIONS], F32)
        for lo, copy in ((0, nc.vector.tensor_copy), (P // 2, nc.scalar.copy)):
            hi = lo + P // 2
            copy(out=result[:, lo:hi, :], in_=planes[:, :, lo:hi].rearrange("b q o -> b o q"))
        nc.sync.dma_start(out=out.rearrange("b o i j -> b (o i j)"), in_=result[:].rearrange("b o q -> b (o q)"))
